import numpy as np
import ml_dtypes


def mxq(x, axis, fmt="e4m3"):
    dtype, down = {"e4m3": (ml_dtypes.float8_e4m3fn, 7), "e5m2": (ml_dtypes.float8_e5m2, 14)}[fmt]
    v = np.moveaxis(np.asarray(x, np.float32).astype(ml_dtypes.bfloat16).astype(np.float64), axis, -1)
    blocks = v.reshape(v.shape[:-1] + (-1, 32))
    amax = np.abs(blocks).max(-1, keepdims=True)
    byte = np.maximum(np.where(amax > 0, np.frexp(amax)[1] - 1 + 127, 0) - down, 1)
    scale = np.exp2(byte - 127.0)
    codes = (blocks / scale).astype(np.float32).astype(dtype).astype(np.float64)
    return np.moveaxis((codes * scale).reshape(v.shape), -1, axis)


WIDE = False


def mx_kscale(k):
    if not WIDE:
        return np.ones(k)
    levels = np.array([10, -10, 5, -5, 0])
    a = np.random.permutation(np.resize(levels, k // 512 * 4)).reshape(k // 512, 4)
    idx = np.arange(k)
    return np.exp2(a[idx // 512, idx % 128 // 32])


BF16 = ml_dtypes.bfloat16


def bf(x):
    return np.asarray(x, np.float32).astype(BF16)


def f64(x):
    return np.asarray(x).astype(np.float64)


B, D, H = 4096, 1024, 512


def setup_inputs():
    s, t = mx_kscale(D), mx_kscale(H)
    return {"x": bf(np.random.standard_normal((B, D)) * s),
            "xz_o": bf(np.random.standard_normal((B, H)) * 0.7),
            "h_prev": bf(np.random.standard_normal((B, H)) * t),
            "c": bf(np.random.standard_normal((B, H)) * 0.65),
            "w_i": bf(np.random.standard_normal((D, H)) * 0.7 / np.sqrt(D) / s[:, None]),
            "w_ho": bf(np.random.standard_normal((H, H)) * 0.7 / np.sqrt(H) / t[:, None]),
            "w_co": bf(np.random.standard_normal((H, H)) * 0.7 / np.sqrt(H)),
            "w_c": bf(np.random.standard_normal((H, H)) * 0.7 / np.sqrt(H)),
            "b_o": bf(np.random.standard_normal(H) * 0.3)}


def reference(x, xz_o, h_prev, c, w_i, w_ho, w_co, w_c, b_o):
    cc = f64(c)
    o = f64(xz_o) + (mxq(f64(h_prev), 1, "e4m3") @ mxq(f64(w_ho), 0, "e4m3")) + (mxq(cc, 1, "e4m3") @ mxq(f64(w_co), 0, "e4m3")) + f64(b_o)
    return np.tanh(o) * ((mxq(np.tanh(cc), 1, "e4m3") @ mxq(f64(w_c), 0, "e4m3")) + (mxq(f64(x), 1, "e4m3") @ mxq(f64(w_i), 0, "e4m3")))

@@ -1,0 +1,302 @@
+from contextlib import ExitStack
+
+import concourse.mybir as mybir
+from concourse.masks import make_identity
+
+F32 = mybir.dt.float32
+BF16 = mybir.dt.bfloat16
+U32 = mybir.dt.uint32
+U8 = mybir.dt.uint8
+FP8X4 = mybir.dt.float8_e4m3fn_x4
+ADD = mybir.AluOpType.add
+MULT = mybir.AluOpType.mult
+TANH = mybir.ActivationFunctionType.Tanh
+
+B, D, H = 4096, 1024, 512
+FLOPS = 2 * B * H * (D + 3 * H)
+
+P = 128
+PACK = 4
+K_PASS = P * PACK
+PAIR = 2
+WORDS = K_PASS // PAIR
+BANK = 512
+CHUNK_TILES = 4
+CHUNKS = B // (P * CHUNK_TILES)
+ROUND_TILES = 2
+ROUNDS = B // (P * ROUND_TILES)
+INPUT_BUFS = 4
+BIAS_AHEAD = 2
+
+W_HO = 0
+W_CO = 1
+W_C = 2
+W_I0 = 3
+W_I1 = 4
+W_PASSES = 5
+
+assert ROUND_TILES * WORDS == BANK
+assert D // PAIR == BANK
+
+
+def tile_residuallstmcell_pb_t_kernel(tc, x, xz_o, h_prev, c, w_i, w_ho, w_co, w_c, b_o, out):
+    nc = tc.nc
+
+    x_chunks = x.rearrange("(n p t) d -> n p (t d)", p=P, t=CHUNK_TILES)
+    xz_chunks = xz_o.rearrange("(n p t) d -> n p (t d)", p=P, t=CHUNK_TILES)
+    h_chunks = h_prev.rearrange("(n p t) d -> n p (t d)", p=P, t=CHUNK_TILES)
+    c_chunks = c.rearrange("(n p t) d -> n p (t d)", p=P, t=CHUNK_TILES)
+    out_chunks = out.rearrange("(n p t) d -> n p (t d)", p=P, t=CHUNK_TILES)
+
+    with ExitStack() as ctx:
+        const = ctx.enter_context(tc.tile_pool(name="const", bufs=1))
+        w_stage = ctx.enter_context(tc.tile_pool(name="w_stage", bufs=3))
+        inputs = ctx.enter_context(tc.tile_pool(name="inputs", bufs=INPUT_BUFS))
+        grouped = ctx.enter_context(tc.tile_pool(name="grouped", bufs=2))
+        quantised = ctx.enter_context(tc.tile_pool(name="quantised", bufs=2))
+        gates = ctx.enter_context(tc.tile_pool(name="gates", bufs=3))
+        results = ctx.enter_context(tc.tile_pool(name="results", bufs=3))
+        psum = ctx.enter_context(tc.psum_pool(name="psum", bufs=2))
+        ctx.enter_context(tc.manual_schedule())
+
+        ident = const.tile([P, P], F32)
+        make_identity(nc, ident[:])
+        warm_in = const.tile([P, 1], F32)
+        warm_out = const.tile([P, 1], F32)
+        ones = const.tile([P, P], BF16)
+        b_row = const.tile([P, H], BF16)
+        nc.vector.memset(b_row[:], 0.0)
+        nc.vector.memset(ones[:], 1.0)
+        nc.vector.memset(warm_in[:], 0.0)
+        nc.scalar.dma_start(out=b_row[0:1, :], in_=b_o.unsqueeze(0))
+        nc.scalar.activation(out=warm_out[:], in_=warm_in[:], func=TANH)
+
+        w_raw = {}
+        for k, rows in (
+            (W_HO, w_ho),
+            (W_CO, w_co),
+            (W_C, w_c),
+            (W_I0, w_i[0:K_PASS, :]),
+            (W_I1, w_i[K_PASS : 2 * K_PASS, :]),
+        ):
+            raw = const.tile([P, PACK * H], BF16, name="w_raw%d" % k)
+            nc.sync.dma_start(
+                out=raw[:].rearrange("q (u ec) -> q u ec", u=2),
+                in_=rows.rearrange("(u q e) c -> q u (e c)", u=2, e=PAIR),
+            )
+            w_raw[k] = raw
+
+        chunk_tiles = {}
+
+        def load_chunk(n, pieces):
+            h_sb = inputs.tile([P, CHUNK_TILES * H], BF16)
+            c_sb = inputs.tile([P, CHUNK_TILES * H], BF16)
+            x_sb = inputs.tile([P, CHUNK_TILES * D], BF16)
+            xz_sb = inputs.tile([P, CHUNK_TILES * H], BF16)
+            for piece in range(pieces):
+                for sb, dram in ((h_sb, h_chunks), (c_sb, c_chunks), (x_sb, x_chunks), (xz_sb, xz_chunks)):
+                    width = sb.shape[1] // pieces
+                    cols = slice(piece * width, (piece + 1) * width)
+                    nc.sync.dma_start(out=sb[:, cols], in_=dram[n, :, cols])
+            chunk_tiles[n] = {"h": h_sb, "c": c_sb, "x": x_sb, "xz": xz_sb}
+
+        load_chunk(0, CHUNK_TILES // ROUND_TILES)
+        for n in range(1, INPUT_BUFS):
+            load_chunk(n, 1)
+
+        w_codes = const.tile([P, W_PASSES * H], U32, align_bytes=64)
+        w_scales = const.tile([P, W_PASSES * H], U8, align_bytes=64)
+        w_grouped = {}
+
+        def regroup_weight(k):
+            wg = w_stage.tile([P, H * PACK], BF16, align_bytes=64)
+            rows = w_raw[k][:].rearrange("p (t c) -> p t c", t=PACK)
+            half = H // 2
+            nc.vector.tensor_copy(
+                out=wg[:, 0 : half * PACK].rearrange("p (c i t) -> p c t i", i=4, t=PACK),
+                in_=rows[:, :, 0:half].rearrange("p t (c i) -> p c t i", i=4),
+            )
+            nc.scalar.copy(
+                out=wg[:, half * PACK : H * PACK].rearrange("p (c i t) -> p c t i", i=4, t=PACK),
+                in_=rows[:, :, half:H].rearrange("p t (c i) -> p c t i", i=4),
+            )
+            w_grouped[k] = wg
+
+        def quantise_weight(k):
+            nc.vector.quantize_mx(
+                out=w_codes[:, k * H : (k + 1) * H].bitcast(FP8X4),
+                scales=w_scales[:, k * H : (k + 1) * H],
+                in_=w_grouped[k][:],
+            )
+
+        regroup_weight(0)
+        for k in range(1, W_PASSES):
+            regroup_weight(k)
+            quantise_weight(k - 1)
+        quantise_weight(W_PASSES - 1)
+
+        bias_bank = psum.tile([P, H], F32, tag="o_bank")
+        nc.tensor.matmul(out=bias_bank[:], lhsT=ones[:], rhs=b_row[:], start=True, stop=True)
+        bias = const.tile([P, H], F32)
+        nc.vector.tensor_copy(out=bias[:], in_=bias_bank[:])
+
+        def where(i, s):
+            return divmod(i * ROUND_TILES + s, CHUNK_TILES)
+
+        banks = {}
+        regrouped = {}
+        codes = {}
+        sums = {}
+        biased = {}
+        gate_in = {}
+        gate = {}
+
+        def add_bias(i):
+            pre = gates.tile([P, ROUND_TILES * H], F32)
+            for s in range(ROUND_TILES):
+                n, t = where(i, s)
+                nc.gpsimd.tensor_tensor(
+                    out=pre[:, s * H : (s + 1) * H],
+                    in0=chunk_tiles[n]["xz"][:, t * H : (t + 1) * H],
+                    in1=bias[:],
+                    op=ADD,
+                )
+            biased[i] = pre
+
+        def transpose_round(i):
+            h_bank = psum.tile([P, BANK], F32, bufs=1)
+            c_bank = psum.tile([P, BANK], F32, bufs=1)
+            for name, bank in (("h", h_bank), ("c", c_bank)):
+                for s in range(ROUND_TILES):
+                    n, t = where(i, s)
+                    words = chunk_tiles[n][name][:].bitcast(F32)
+                    for u in range(WORDS // P):
+                        nc.tensor.transpose(
+                            bank[:, s * WORDS + u * P : s * WORDS + (u + 1) * P],
+                            words[:, t * WORDS + u * P : t * WORDS + (u + 1) * P],
+                            ident[:],
+                        )
+            x_banks = []
+            for s in range(ROUND_TILES):
+                n, t = where(i, s)
+                words = chunk_tiles[n]["x"][:].bitcast(F32)
+                x_bank = psum.tile([P, BANK], F32)
+                for j in range(BANK // P):
+                    nc.tensor.transpose(
+                        x_bank[:, j * P : (j + 1) * P],
+                        words[:, t * BANK + j * P : t * BANK + (j + 1) * P],
+                        ident[:],
+                    )
+                x_banks.append(x_bank)
+            banks[i] = {"h": h_bank, "c": c_bank, "x": x_banks}
+
+        def interleave(copy, dst_words, bank):
+            copy(
+                out=dst_words.rearrange("p (a r u) -> p a r u", a=2, u=2),
+                in_=bank[:].rearrange("p (a u r) -> p a r u", a=2, u=2),
+            )
+
+        def empty_round(i):
+            hc_grouped = grouped.tile([P, 2 * ROUND_TILES * K_PASS], BF16, align_bytes=64)
+            t_grouped = grouped.tile([P, ROUND_TILES * K_PASS], BF16, align_bytes=64)
+            x_grouped = grouped.tile([P, ROUND_TILES * D], BF16, align_bytes=64)
+            hc_words = hc_grouped[:].bitcast(F32)
+            x_words = x_grouped[:].bitcast(F32)
+            interleave(nc.scalar.copy, hc_words[:, 0:BANK], banks[i]["h"])
+            interleave(nc.scalar.copy, hc_words[:, BANK : 2 * BANK], banks[i]["c"])
+            interleave(nc.vector.tensor_copy, x_words[:, BANK : 2 * BANK], banks[i]["x"][1])
+            c_values = banks[i]["c"][:].bitcast(BF16)
+            for s in range(ROUND_TILES):
+                nc.scalar.activation(
+                    out=t_grouped[:, s * K_PASS : (s + 1) * K_PASS].rearrange("p (r u e) -> p r u e", u=2, e=PAIR),
+                    in_=c_values[:, s * K_PASS : (s + 1) * K_PASS].rearrange("p (u r e) -> p r u e", u=2, e=PAIR),
+                    func=TANH,
+                )
+            interleave(nc.scalar.copy, x_words[:, 0:BANK], banks[i]["x"][0])
+            regrouped[i] = {"hc": hc_grouped, "t": t_grouped, "x": x_grouped}
+
+        def quantise_round(i):
+            made = {}
+            for name in ("hc", "t", "x"):
+                values = regrouped[i][name]
+                width = values.shape[1] // PACK
+                words = quantised.tile([P, width], U32, name=name + "_codes", align_bytes=64)
+                scales = quantised.tile([P, width], U8, name=name + "_scales", align_bytes=64)
+                nc.vector.quantize_mx(out=words[:].bitcast(FP8X4), scales=scales[:], in_=values[:])
+                made[name] = (words, scales)
+            codes[i] = made
+
+        def mx_pass(bank, operand, block, k, start, stop):
+            words, scales = operand
+            rows = slice(block * P, (block + 1) * P)
+            cols = slice(k * H, (k + 1) * H)
+            nc.tensor.matmul_mx(
+                out=bank[:],
+                lhsT=words[:, rows].bitcast(FP8X4),
+                lhsT_scale=scales[:, rows],
+                rhs=w_codes[:, cols].bitcast(FP8X4),
+                rhs_scale=w_scales[:, cols],
+                start=start,
+                stop=stop,
+            )
+
+        def multiply_round(i):
+            o_banks = []
+            r_banks = []
+            for s in range(ROUND_TILES):
+                o_bank = psum.tile([P, H], F32)
+                mx_pass(o_bank, codes[i]["hc"], s, W_HO, True, False)
+                mx_pass(o_bank, codes[i]["hc"], ROUND_TILES + s, W_CO, False, True)
+                o_banks.append(o_bank)
+            for s in range(ROUND_TILES):
+                r_bank = psum.tile([P, H], F32)
+                mx_pass(r_bank, codes[i]["t"], s, W_C, True, False)
+                mx_pass(r_bank, codes[i]["x"], 2 * s, W_I0, False, False)
+                mx_pass(r_bank, codes[i]["x"], 2 * s + 1, W_I1, False, True)
+                r_banks.append(r_bank)
+            sums[i] = {"o": o_banks, "r": r_banks}
+
+        def sum_gate_input(i):
+            o_sum = gates.tile([P, ROUND_TILES * H], F32)
+            for s in range(ROUND_TILES):
+                cols = slice(s * H, (s + 1) * H)
+                nc.vector.tensor_tensor(out=o_sum[:, cols], in0=sums[i]["o"][s][:], in1=biased[i][:, cols], op=ADD)
+            gate_in[i] = o_sum
+
+        def squash_gate(i):
+            tanh_o = gates.tile([P, ROUND_TILES * H], F32)
+            for s in range(ROUND_TILES):
+                cols = slice(s * H, (s + 1) * H)
+                nc.scalar.activation(out=tanh_o[:, cols], in_=gate_in[i][:, cols], func=TANH)
+            gate[i] = tanh_o
+
+        def finish_round(i):
+            product = results.tile([P, ROUND_TILES * H], F32)
+            for s in range(ROUND_TILES):
+                cols = slice(s * H, (s + 1) * H)
+                nc.vector.tensor_tensor(out=product[:, cols], in0=sums[i]["r"][s][:], in1=gate[i][:, cols], op=MULT)
+            n, t = where(i, 0)
+            nc.sync.dma_start(out=out_chunks[n, :, t * H : (t + ROUND_TILES) * H], in_=product[:])
+
+        for i in range(BIAS_AHEAD):
+            add_bias(i)
+        transpose_round(0)
+        empty_round(0)
+        quantise_round(0)
+        for i in range(ROUNDS):
+            following = i + 1
+            if following < ROUNDS:
+                transpose_round(following)
+            n, t = where(following, ROUND_TILES - 1)
+            if t == CHUNK_TILES - 1 and n + INPUT_BUFS < CHUNKS:
+                load_chunk(n + INPUT_BUFS, 1)
+            multiply_round(i)
+            if following < ROUNDS:
+                empty_round(following)
+            sum_gate_input(i)
+            if following < ROUNDS:
+                quantise_round(following)
+            squash_gate(i)
+            finish_round(i)
+            if i + BIAS_AHEAD < ROUNDS:
+                add_bias(i + BIAS_AHEAD)

@@ -55,7 +55,7 @@ def tile_residuallstmcell_pb_t_kernel(tc, x, xz_o, h_prev, c, w_i, w_ho, w_co, w
         grouped = ctx.enter_context(tc.tile_pool(name="grouped", bufs=2))
         quantised = ctx.enter_context(tc.tile_pool(name="quantised", bufs=2))
         gates = ctx.enter_context(tc.tile_pool(name="gates", bufs=3))
-        results = ctx.enter_context(tc.tile_pool(name="results", bufs=3))
+        results = ctx.enter_context(tc.tile_pool(name="results", bufs=6))
         psum = ctx.enter_context(tc.psum_pool(name="psum", bufs=2))
         ctx.enter_context(tc.manual_schedule())
 

@@ -68,41 +68,61 @@ def tile_residuallstmcell_pb_t_kernel(tc, x, xz_o, h_prev, c, w_i, w_ho, w_co, w
         nc.vector.memset(b_row[:], 0.0)
         nc.vector.memset(ones[:], 1.0)
         nc.vector.memset(warm_in[:], 0.0)
-        nc.scalar.dma_start(out=b_row[0:1, :], in_=b_o.unsqueeze(0))
         nc.scalar.activation(out=warm_out[:], in_=warm_in[:], func=TANH)
 
+        w_rows = {
+            W_HO: w_ho,
+            W_CO: w_co,
+            W_C: w_c,
+            W_I0: w_i[0:K_PASS, :],
+            W_I1: w_i[K_PASS : 2 * K_PASS, :],
+        }
         w_raw = {}
-        for k, rows in (
-            (W_HO, w_ho),
-            (W_CO, w_co),
-            (W_C, w_c),
-            (W_I0, w_i[0:K_PASS, :]),
-            (W_I1, w_i[K_PASS : 2 * K_PASS, :]),
-        ):
+
+        def load_weight(k):
             raw = const.tile([P, PACK * H], BF16, name="w_raw%d" % k)
             nc.sync.dma_start(
                 out=raw[:].rearrange("q (u ec) -> q u ec", u=2),
-                in_=rows.rearrange("(u q e) c -> q u (e c)", u=2, e=PAIR),
+                in_=w_rows[k].rearrange("(u q e) c -> q u (e c)", u=2, e=PAIR),
             )
             w_raw[k] = raw
 
         chunk_tiles = {}
 
-        def load_chunk(n, pieces):
+        def make_chunk(n):
             h_sb = inputs.tile([P, CHUNK_TILES * H], BF16)
             c_sb = inputs.tile([P, CHUNK_TILES * H], BF16)
             x_sb = inputs.tile([P, CHUNK_TILES * D], BF16)
             xz_sb = inputs.tile([P, CHUNK_TILES * H], BF16)
-            for piece in range(pieces):
-                for sb, dram in ((h_sb, h_chunks), (c_sb, c_chunks), (x_sb, x_chunks), (xz_sb, xz_chunks)):
-                    width = sb.shape[1] // pieces
-                    cols = slice(piece * width, (piece + 1) * width)
-                    nc.sync.dma_start(out=sb[:, cols], in_=dram[n, :, cols])
             chunk_tiles[n] = {"h": h_sb, "c": c_sb, "x": x_sb, "xz": xz_sb}
 
-        load_chunk(0, CHUNK_TILES // ROUND_TILES)
+        chunks = {"h": h_chunks, "c": c_chunks, "x": x_chunks, "xz": xz_chunks}
+
+        def load_piece(n, name, piece, pieces):
+            sb = chunk_tiles[n][name]
+            width = sb.shape[1] // pieces
+            cols = slice(piece * width, (piece + 1) * width)
+            nc.sync.dma_start(out=sb[:, cols], in_=chunks[name][n, :, cols])
+
+        def load_chunk(n):
+            make_chunk(n)
+            for name in ("h", "c", "x", "xz"):
+                load_piece(n, name, 0, 1)
+
+        load_weight(W_HO)
+        load_weight(W_CO)
+        make_chunk(0)
+        for name in ("h", "c", "x"):
+            load_piece(0, name, 0, 2)
+        nc.sync.dma_start(out=b_row[0:1, :], in_=b_o.unsqueeze(0))
+        load_weight(W_C)
+        load_weight(W_I0)
+        load_weight(W_I1)
+        load_piece(0, "xz", 0, 2)
+        for name in ("h", "c", "x", "xz"):
+            load_piece(0, name, 1, 2)
         for n in range(1, INPUT_BUFS):
-            load_chunk(n, 1)
+            load_chunk(n)
 
         w_codes = const.tile([P, W_PASSES * H], U32, align_bytes=64)
         w_scales = const.tile([P, W_PASSES * H], U8, align_bytes=64)
@@ -129,16 +149,7 @@ def tile_residuallstmcell_pb_t_kernel(tc, x, xz_o, h_prev, c, w_i, w_ho, w_co, w
                 in_=w_grouped[k][:],
             )
 
-        regroup_weight(0)
-        for k in range(1, W_PASSES):
-            regroup_weight(k)
-            quantise_weight(k - 1)
-        quantise_weight(W_PASSES - 1)
-
-        bias_bank = psum.tile([P, H], F32, tag="o_bank")
-        nc.tensor.matmul(out=bias_bank[:], lhsT=ones[:], rhs=b_row[:], start=True, stop=True)
         bias = const.tile([P, H], F32)
-        nc.vector.tensor_copy(out=bias[:], in_=bias_bank[:])
 
         def where(i, s):
             return divmod(i * ROUND_TILES + s, CHUNK_TILES)
@@ -204,7 +215,8 @@ def tile_residuallstmcell_pb_t_kernel(tc, x, xz_o, h_prev, c, w_i, w_ho, w_co, w
             x_words = x_grouped[:].bitcast(F32)
             interleave(nc.scalar.copy, hc_words[:, 0:BANK], banks[i]["h"])
             interleave(nc.scalar.copy, hc_words[:, BANK : 2 * BANK], banks[i]["c"])
-            interleave(nc.vector.tensor_copy, x_words[:, BANK : 2 * BANK], banks[i]["x"][1])
+            if i % 2 == 0:
+                interleave(nc.vector.tensor_copy, x_words[:, BANK : 2 * BANK], banks[i]["x"][1])
             c_values = banks[i]["c"][:].bitcast(BF16)
             for s in range(ROUND_TILES):
                 nc.scalar.activation(
@@ -213,18 +225,21 @@ def tile_residuallstmcell_pb_t_kernel(tc, x, xz_o, h_prev, c, w_i, w_ho, w_co, w
                     func=TANH,
                 )
             interleave(nc.scalar.copy, x_words[:, 0:BANK], banks[i]["x"][0])
+            if i % 2 == 1:
+                interleave(nc.scalar.copy, x_words[:, BANK : 2 * BANK], banks[i]["x"][1])
             regrouped[i] = {"hc": hc_grouped, "t": t_grouped, "x": x_grouped}
 
+        def quantise_rows(i, name):
+            values = regrouped[i][name]
+            width = values.shape[1] // PACK
+            words = quantised.tile([P, width], U32, name=name + "_codes", align_bytes=64)
+            scales = quantised.tile([P, width], U8, name=name + "_scales", align_bytes=64)
+            nc.vector.quantize_mx(out=words[:].bitcast(FP8X4), scales=scales[:], in_=values[:])
+            codes.setdefault(i, {})[name] = (words, scales)
+
         def quantise_round(i):
-            made = {}
             for name in ("hc", "t", "x"):
-                values = regrouped[i][name]
-                width = values.shape[1] // PACK
-                words = quantised.tile([P, width], U32, name=name + "_codes", align_bytes=64)
-                scales = quantised.tile([P, width], U8, name=name + "_scales", align_bytes=64)
-                nc.vector.quantize_mx(out=words[:].bitcast(FP8X4), scales=scales[:], in_=values[:])
-                made[name] = (words, scales)
-            codes[i] = made
+                quantise_rows(i, name)
 
         def mx_pass(bank, operand, block, k, start, stop):
             words, scales = operand
@@ -278,18 +293,33 @@ def tile_residuallstmcell_pb_t_kernel(tc, x, xz_o, h_prev, c, w_i, w_ho, w_co, w
             n, t = where(i, 0)
             nc.sync.dma_start(out=out_chunks[n, :, t * H : (t + ROUND_TILES) * H], in_=product[:])
 
+        regroup_weight(W_HO)
+        regroup_weight(W_CO)
+        quantise_weight(W_HO)
+        quantise_weight(W_CO)
+        transpose_round(0)
+        bias_bank = psum.tile([P, H], F32, tag="o_bank")
+        nc.tensor.matmul(out=bias_bank[:], lhsT=ones[:], rhs=b_row[:], start=True, stop=True)
+        empty_round(0)
+        nc.scalar.copy(out=bias[:], in_=bias_bank[:])
+        quantise_rows(0, "hc")
+        regroup_weight(W_C)
+        quantise_rows(0, "t")
+        regroup_weight(W_I0)
+        quantise_weight(W_C)
+        quantise_rows(0, "x")
+        regroup_weight(W_I1)
+        quantise_weight(W_I0)
+        quantise_weight(W_I1)
         for i in range(BIAS_AHEAD):
             add_bias(i)
-        transpose_round(0)
-        empty_round(0)
-        quantise_round(0)
         for i in range(ROUNDS):
             following = i + 1
             if following < ROUNDS:
                 transpose_round(following)
             n, t = where(following, ROUND_TILES - 1)
             if t == CHUNK_TILES - 1 and n + INPUT_BUFS < CHUNKS:
-                load_chunk(n + INPUT_BUFS, 1)
+                load_chunk(n + INPUT_BUFS)
             multiply_round(i)
             if following < ROUNDS:
                 empty_round(following)

@@ -124,8 +124,8 @@ def tile_residuallstmcell_pb_t_kernel(tc, x, xz_o, h_prev, c, w_i, w_ho, w_co, w
         for n in range(1, INPUT_BUFS):
             load_chunk(n)
 
-        w_codes = const.tile([P, W_PASSES * H], U32, align_bytes=64)
-        w_scales = const.tile([P, W_PASSES * H], U8, align_bytes=64)
+        w_codes = const.tile([P, W_PASSES * H], U32, align_bytes=256)
+        w_scales = const.tile([P, W_PASSES * H], U8, align_bytes=256)
         w_grouped = {}
 
         def regroup_weight(k):
@@ -183,7 +183,7 @@ def tile_residuallstmcell_pb_t_kernel(tc, x, xz_o, h_prev, c, w_i, w_ho, w_co, w
                     words = chunk_tiles[n][name][:].bitcast(F32)
                     for u in range(WORDS // P):
                         nc.tensor.transpose(
-                            bank[:, s * WORDS + u * P : s * WORDS + (u + 1) * P],
+                            bank[:, (u * ROUND_TILES + s) * P : (u * ROUND_TILES + s + 1) * P],
                             words[:, t * WORDS + u * P : t * WORDS + (u + 1) * P],
                             ident[:],
                         )
@@ -194,7 +194,7 @@ def tile_residuallstmcell_pb_t_kernel(tc, x, xz_o, h_prev, c, w_i, w_ho, w_co, w
                 x_bank = psum.tile([P, BANK], F32)
                 for j in range(BANK // P):
                     nc.tensor.transpose(
-                        x_bank[:, j * P : (j + 1) * P],
+                        x_bank[:, (j % 2 * 2 + j // 2) * P : (j % 2 * 2 + j // 2 + 1) * P],
                         words[:, t * BANK + j * P : t * BANK + (j + 1) * P],
                         ident[:],
                     )
@@ -203,8 +203,8 @@ def tile_residuallstmcell_pb_t_kernel(tc, x, xz_o, h_prev, c, w_i, w_ho, w_co, w
 
         def interleave(copy, dst_words, bank):
             copy(
-                out=dst_words.rearrange("p (a r u) -> p a r u", a=2, u=2),
-                in_=bank[:].rearrange("p (a u r) -> p a r u", a=2, u=2),
+                out=dst_words.rearrange("p (w u) -> p w u", u=2),
+                in_=bank[:].rearrange("p (u w) -> p w u", u=2),
             )
 
         def empty_round(i):
@@ -217,13 +217,11 @@ def tile_residuallstmcell_pb_t_kernel(tc, x, xz_o, h_prev, c, w_i, w_ho, w_co, w
             interleave(nc.scalar.copy, hc_words[:, BANK : 2 * BANK], banks[i]["c"])
             if i % 2 == 0:
                 interleave(nc.vector.tensor_copy, x_words[:, BANK : 2 * BANK], banks[i]["x"][1])
-            c_values = banks[i]["c"][:].bitcast(BF16)
-            for s in range(ROUND_TILES):
-                nc.scalar.activation(
-                    out=t_grouped[:, s * K_PASS : (s + 1) * K_PASS].rearrange("p (r u e) -> p r u e", u=2, e=PAIR),
-                    in_=c_values[:, s * K_PASS : (s + 1) * K_PASS].rearrange("p (u r e) -> p r u e", u=2, e=PAIR),
-                    func=TANH,
-                )
+            nc.scalar.activation(
+                out=t_grouped[:].rearrange("p (w u e) -> p w u e", u=2, e=PAIR),
+                in_=banks[i]["c"][:].bitcast(BF16).rearrange("p (u w e) -> p w u e", u=2, e=PAIR),
+                func=TANH,
+            )
             interleave(nc.scalar.copy, x_words[:, 0:BANK], banks[i]["x"][0])
             if i % 2 == 1:
                 interleave(nc.scalar.copy, x_words[:, BANK : 2 * BANK], banks[i]["x"][1])
@@ -232,8 +230,8 @@ def tile_residuallstmcell_pb_t_kernel(tc, x, xz_o, h_prev, c, w_i, w_ho, w_co, w
         def quantise_rows(i, name):
             values = regrouped[i][name]
             width = values.shape[1] // PACK
-            words = quantised.tile([P, width], U32, name=name + "_codes", align_bytes=64)
-            scales = quantised.tile([P, width], U8, name=name + "_scales", align_bytes=64)
+            words = quantised.tile([P, width], U32, name=name + "_codes", align_bytes=256)
+            scales = quantised.tile([P, width], U8, name=name + "_scales", align_bytes=256)
             nc.vector.quantize_mx(out=words[:].bitcast(FP8X4), scales=scales[:], in_=values[:])
             codes.setdefault(i, {})[name] = (words, scales)
 

@@ -26,6 +26,7 @@ CHUNKS = B // (P * CHUNK_TILES)
 ROUND_TILES = 2
 ROUNDS = B // (P * ROUND_TILES)
 INPUT_BUFS = 4
+W_VECTOR_COLS = 320
 BIAS_AHEAD = 2
 
 W_HO = 0
@@ -122,7 +123,10 @@ def tile_residuallstmcell_pb_t_kernel(tc, x, xz_o, h_prev, c, w_i, w_ho, w_co, w
         for name in ("h", "c", "x", "xz"):
             load_piece(0, name, 1, 2)
         for n in range(1, INPUT_BUFS):
-            load_chunk(n)
+            make_chunk(n)
+            for piece in range(CHUNK_TILES // ROUND_TILES):
+                for name in ("h", "c", "x", "xz"):
+                    load_piece(n, name, piece, CHUNK_TILES // ROUND_TILES)
 
         w_codes = const.tile([P, W_PASSES * H], U32, align_bytes=256)
         w_scales = const.tile([P, W_PASSES * H], U8, align_bytes=256)
@@ -131,14 +135,13 @@ def tile_residuallstmcell_pb_t_kernel(tc, x, xz_o, h_prev, c, w_i, w_ho, w_co, w
         def regroup_weight(k):
             wg = w_stage.tile([P, H * PACK], BF16, align_bytes=64)
             rows = w_raw[k][:].rearrange("p (t c) -> p t c", t=PACK)
-            half = H // 2
             nc.vector.tensor_copy(
-                out=wg[:, 0 : half * PACK].rearrange("p (c i t) -> p c t i", i=4, t=PACK),
-                in_=rows[:, :, 0:half].rearrange("p t (c i) -> p c t i", i=4),
+                out=wg[:, 0 : W_VECTOR_COLS * PACK].rearrange("p (c i t) -> p c t i", i=4, t=PACK),
+                in_=rows[:, :, 0:W_VECTOR_COLS].rearrange("p t (c i) -> p c t i", i=4),
             )
             nc.scalar.copy(
-                out=wg[:, half * PACK : H * PACK].rearrange("p (c i t) -> p c t i", i=4, t=PACK),
-                in_=rows[:, :, half:H].rearrange("p t (c i) -> p c t i", i=4),
+                out=wg[:, W_VECTOR_COLS * PACK : H * PACK].rearrange("p (c i t) -> p c t i", i=4, t=PACK),
+                in_=rows[:, :, W_VECTOR_COLS:H].rearrange("p t (c i) -> p c t i", i=4),
             )
             w_grouped[k] = wg
 
@@ -207,25 +210,29 @@ def tile_residuallstmcell_pb_t_kernel(tc, x, xz_o, h_prev, c, w_i, w_ho, w_co, w
                 in_=bank[:].rearrange("p (u w) -> p w u", u=2),
             )
 
-        def empty_round(i):
+        def empty_gate_banks(i, copy_h):
             hc_grouped = grouped.tile([P, 2 * ROUND_TILES * K_PASS], BF16, align_bytes=64)
-            t_grouped = grouped.tile([P, ROUND_TILES * K_PASS], BF16, align_bytes=64)
-            x_grouped = grouped.tile([P, ROUND_TILES * D], BF16, align_bytes=64)
             hc_words = hc_grouped[:].bitcast(F32)
-            x_words = x_grouped[:].bitcast(F32)
-            interleave(nc.scalar.copy, hc_words[:, 0:BANK], banks[i]["h"])
+            interleave(copy_h, hc_words[:, 0:BANK], banks[i]["h"])
             interleave(nc.scalar.copy, hc_words[:, BANK : 2 * BANK], banks[i]["c"])
-            if i % 2 == 0:
-                interleave(nc.vector.tensor_copy, x_words[:, BANK : 2 * BANK], banks[i]["x"][1])
+            regrouped[i] = {"hc": hc_grouped}
+
+        def empty_tanh_c(i):
+            t_grouped = grouped.tile([P, ROUND_TILES * K_PASS], BF16, align_bytes=64)
             nc.scalar.activation(
                 out=t_grouped[:].rearrange("p (w u e) -> p w u e", u=2, e=PAIR),
                 in_=banks[i]["c"][:].bitcast(BF16).rearrange("p (u w e) -> p w u e", u=2, e=PAIR),
                 func=TANH,
             )
+            regrouped[i]["t"] = t_grouped
+
+        def empty_x_banks(i):
+            x_grouped = grouped.tile([P, ROUND_TILES * D], BF16, align_bytes=64)
+            x_words = x_grouped[:].bitcast(F32)
             interleave(nc.scalar.copy, x_words[:, 0:BANK], banks[i]["x"][0])
-            if i % 2 == 1:
-                interleave(nc.scalar.copy, x_words[:, BANK : 2 * BANK], banks[i]["x"][1])
-            regrouped[i] = {"hc": hc_grouped, "t": t_grouped, "x": x_grouped}
+            copy = nc.vector.tensor_copy if i % 2 == 0 else nc.scalar.copy
+            interleave(copy, x_words[:, BANK : 2 * BANK], banks[i]["x"][1])
+            regrouped[i]["x"] = x_grouped
 
         def quantise_rows(i, name):
             values = regrouped[i][name]
@@ -253,21 +260,24 @@ def tile_residuallstmcell_pb_t_kernel(tc, x, xz_o, h_prev, c, w_i, w_ho, w_co, w
                 stop=stop,
             )
 
-        def multiply_round(i):
+        def multiply_gate(i):
             o_banks = []
-            r_banks = []
             for s in range(ROUND_TILES):
                 o_bank = psum.tile([P, H], F32)
                 mx_pass(o_bank, codes[i]["hc"], s, W_HO, True, False)
                 mx_pass(o_bank, codes[i]["hc"], ROUND_TILES + s, W_CO, False, True)
                 o_banks.append(o_bank)
+            sums[i] = {"o": o_banks}
+
+        def multiply_projections(i):
+            r_banks = []
             for s in range(ROUND_TILES):
                 r_bank = psum.tile([P, H], F32)
                 mx_pass(r_bank, codes[i]["t"], s, W_C, True, False)
                 mx_pass(r_bank, codes[i]["x"], 2 * s, W_I0, False, False)
                 mx_pass(r_bank, codes[i]["x"], 2 * s + 1, W_I1, False, True)
                 r_banks.append(r_bank)
-            sums[i] = {"o": o_banks, "r": r_banks}
+            sums[i]["r"] = r_banks
 
         def sum_gate_input(i):
             o_sum = gates.tile([P, ROUND_TILES * H], F32)
@@ -296,12 +306,15 @@ def tile_residuallstmcell_pb_t_kernel(tc, x, xz_o, h_prev, c, w_i, w_ho, w_co, w
         quantise_weight(W_HO)
         quantise_weight(W_CO)
         transpose_round(0)
-        bias_bank = psum.tile([P, H], F32, tag="o_bank")
+        bias_bank = psum.tile([P, H], F32, tag="r_bank")
         nc.tensor.matmul(out=bias_bank[:], lhsT=ones[:], rhs=b_row[:], start=True, stop=True)
-        empty_round(0)
-        nc.scalar.copy(out=bias[:], in_=bias_bank[:])
+        empty_gate_banks(0, nc.vector.tensor_copy)
         quantise_rows(0, "hc")
+        multiply_gate(0)
+        empty_tanh_c(0)
         regroup_weight(W_C)
+        empty_x_banks(0)
+        nc.scalar.copy(out=bias[:], in_=bias_bank[:])
         quantise_rows(0, "t")
         regroup_weight(W_I0)
         quantise_weight(W_C)
@@ -318,9 +331,13 @@ def tile_residuallstmcell_pb_t_kernel(tc, x, xz_o, h_prev, c, w_i, w_ho, w_co, w
             n, t = where(following, ROUND_TILES - 1)
             if t == CHUNK_TILES - 1 and n + INPUT_BUFS < CHUNKS:
                 load_chunk(n + INPUT_BUFS)
-            multiply_round(i)
+            if i > 0:
+                multiply_gate(i)
+            multiply_projections(i)
             if following < ROUNDS:
-                empty_round(following)
+                empty_gate_banks(following, nc.scalar.copy)
+                empty_tanh_c(following)
+                empty_x_banks(following)
             sum_gate_input(i)
             if following < ROUNDS:
                 quantise_round(following)

@@ -217,20 +217,17 @@ def tile_residuallstmcell_pb_t_kernel(tc, x, xz_o, h_prev, c, w_i, w_ho, w_co, w
             interleave(nc.scalar.copy, hc_words[:, BANK : 2 * BANK], banks[i]["c"])
             regrouped[i] = {"hc": hc_grouped}
 
-        def empty_tanh_c(i):
+        def take_tanh_c(i):
             t_grouped = grouped.tile([P, ROUND_TILES * K_PASS], BF16, align_bytes=64)
-            nc.scalar.activation(
-                out=t_grouped[:].rearrange("p (w u e) -> p w u e", u=2, e=PAIR),
-                in_=banks[i]["c"][:].bitcast(BF16).rearrange("p (u w e) -> p w u e", u=2, e=PAIR),
-                func=TANH,
-            )
+            c_values = regrouped[i]["hc"][:, ROUND_TILES * K_PASS : 2 * ROUND_TILES * K_PASS]
+            nc.scalar.activation(out=t_grouped[:], in_=c_values, func=TANH)
             regrouped[i]["t"] = t_grouped
 
         def empty_x_banks(i):
             x_grouped = grouped.tile([P, ROUND_TILES * D], BF16, align_bytes=64)
             x_words = x_grouped[:].bitcast(F32)
             interleave(nc.scalar.copy, x_words[:, 0:BANK], banks[i]["x"][0])
-            copy = nc.vector.tensor_copy if i % 2 == 0 else nc.scalar.copy
+            copy = nc.vector.tensor_copy if i % 4 == 0 else nc.scalar.copy
             interleave(copy, x_words[:, BANK : 2 * BANK], banks[i]["x"][1])
             regrouped[i]["x"] = x_grouped
 
@@ -243,7 +240,7 @@ def tile_residuallstmcell_pb_t_kernel(tc, x, xz_o, h_prev, c, w_i, w_ho, w_co, w
             codes.setdefault(i, {})[name] = (words, scales)
 
         def quantise_round(i):
-            for name in ("hc", "t", "x"):
+            for name in ("hc", "x", "t"):
                 quantise_rows(i, name)
 
         def mx_pass(bank, operand, block, k, start, stop):
@@ -273,9 +270,9 @@ def tile_residuallstmcell_pb_t_kernel(tc, x, xz_o, h_prev, c, w_i, w_ho, w_co, w
             r_banks = []
             for s in range(ROUND_TILES):
                 r_bank = psum.tile([P, H], F32)
-                mx_pass(r_bank, codes[i]["t"], s, W_C, True, False)
-                mx_pass(r_bank, codes[i]["x"], 2 * s, W_I0, False, False)
-                mx_pass(r_bank, codes[i]["x"], 2 * s + 1, W_I1, False, True)
+                mx_pass(r_bank, codes[i]["x"], 2 * s, W_I0, True, False)
+                mx_pass(r_bank, codes[i]["x"], 2 * s + 1, W_I1, False, False)
+                mx_pass(r_bank, codes[i]["t"], s, W_C, False, True)
                 r_banks.append(r_bank)
             sums[i]["r"] = r_banks
 
@@ -311,7 +308,7 @@ def tile_residuallstmcell_pb_t_kernel(tc, x, xz_o, h_prev, c, w_i, w_ho, w_co, w
         empty_gate_banks(0, nc.vector.tensor_copy)
         quantise_rows(0, "hc")
         multiply_gate(0)
-        empty_tanh_c(0)
+        take_tanh_c(0)
         regroup_weight(W_C)
         empty_x_banks(0)
         nc.scalar.copy(out=bias[:], in_=bias_bank[:])
@@ -336,8 +333,8 @@ def tile_residuallstmcell_pb_t_kernel(tc, x, xz_o, h_prev, c, w_i, w_ho, w_co, w
             multiply_projections(i)
             if following < ROUNDS:
                 empty_gate_banks(following, nc.scalar.copy)
-                empty_tanh_c(following)
                 empty_x_banks(following)
+                take_tanh_c(following)
             sum_gate_input(i)
             if following < ROUNDS:
                 quantise_round(following)

@@ -122,11 +122,12 @@ def tile_residuallstmcell_pb_t_kernel(tc, x, xz_o, h_prev, c, w_i, w_ho, w_co, w
         load_piece(0, "xz", 0, 2)
         for name in ("h", "c", "x", "xz"):
             load_piece(0, name, 1, 2)
-        for n in range(1, INPUT_BUFS):
-            make_chunk(n)
-            for piece in range(CHUNK_TILES // ROUND_TILES):
-                for name in ("h", "c", "x", "xz"):
-                    load_piece(n, name, piece, CHUNK_TILES // ROUND_TILES)
+        make_chunk(1)
+        for piece in range(2):
+            for name in ("h", "c", "x", "xz"):
+                load_piece(1, name, piece, 2)
+        for n in range(2, INPUT_BUFS):
+            load_chunk(n)
 
         w_codes = const.tile([P, W_PASSES * H], U32, align_bytes=256)
         w_scales = const.tile([P, W_PASSES * H], U8, align_bytes=256)
@@ -292,11 +293,17 @@ def tile_residuallstmcell_pb_t_kernel(tc, x, xz_o, h_prev, c, w_i, w_ho, w_co, w
 
         def finish_round(i):
             product = results.tile([P, ROUND_TILES * H], F32)
+            n, t = where(i, 0)
+            tiles_a_store = 1 if i == ROUNDS - 1 else ROUND_TILES
             for s in range(ROUND_TILES):
                 cols = slice(s * H, (s + 1) * H)
                 nc.vector.tensor_tensor(out=product[:, cols], in0=sums[i]["r"][s][:], in1=gate[i][:, cols], op=MULT)
-            n, t = where(i, 0)
-            nc.sync.dma_start(out=out_chunks[n, :, t * H : (t + ROUND_TILES) * H], in_=product[:])
+                if (s + 1) % tiles_a_store == 0:
+                    first = s + 1 - tiles_a_store
+                    nc.sync.dma_start(
+                        out=out_chunks[n, :, (t + first) * H : (t + s + 1) * H],
+                        in_=product[:, first * H : (s + 1) * H],
+                    )
 
         regroup_weight(W_HO)
         regroup_weight(W_CO)

from contextlib import ExitStack

import concourse.mybir as mybir
from concourse.masks import make_identity

F32 = mybir.dt.float32
BF16 = mybir.dt.bfloat16
U32 = mybir.dt.uint32
U8 = mybir.dt.uint8
FP8X4 = mybir.dt.float8_e4m3fn_x4
ADD = mybir.AluOpType.add
MULT = mybir.AluOpType.mult
TANH = mybir.ActivationFunctionType.Tanh

B, D, H = 4096, 1024, 512
FLOPS = 2 * B * H * (D + 3 * H)

P = 128
PACK = 4
K_PASS = P * PACK
PAIR = 2
WORDS = K_PASS // PAIR
BANK = 512
CHUNK_TILES = 4
CHUNKS = B // (P * CHUNK_TILES)
ROUND_TILES = 2
ROUNDS = B // (P * ROUND_TILES)
INPUT_BUFS = 4
W_VECTOR_COLS = 320
BIAS_AHEAD = 2

W_HO = 0
W_CO = 1
W_C = 2
W_I0 = 3
W_I1 = 4
W_PASSES = 5

assert ROUND_TILES * WORDS == BANK
assert D // PAIR == BANK


def tile_residuallstmcell_pb_t_kernel(tc, x, xz_o, h_prev, c, w_i, w_ho, w_co, w_c, b_o, out):
    nc = tc.nc

    x_chunks = x.rearrange("(n p t) d -> n p (t d)", p=P, t=CHUNK_TILES)
    xz_chunks = xz_o.rearrange("(n p t) d -> n p (t d)", p=P, t=CHUNK_TILES)
    h_chunks = h_prev.rearrange("(n p t) d -> n p (t d)", p=P, t=CHUNK_TILES)
    c_chunks = c.rearrange("(n p t) d -> n p (t d)", p=P, t=CHUNK_TILES)
    out_chunks = out.rearrange("(n p t) d -> n p (t d)", p=P, t=CHUNK_TILES)

    with ExitStack() as ctx:
        const = ctx.enter_context(tc.tile_pool(name="const", bufs=1))
        w_stage = ctx.enter_context(tc.tile_pool(name="w_stage", bufs=3))
        inputs = ctx.enter_context(tc.tile_pool(name="inputs", bufs=INPUT_BUFS))
        grouped = ctx.enter_context(tc.tile_pool(name="grouped", bufs=2))
        quantised = ctx.enter_context(tc.tile_pool(name="quantised", bufs=2))
        gates = ctx.enter_context(tc.tile_pool(name="gates", bufs=3))
        results = ctx.enter_context(tc.tile_pool(name="results", bufs=6))
        psum = ctx.enter_context(tc.psum_pool(name="psum", bufs=2))
        ctx.enter_context(tc.manual_schedule())

        ident = const.tile([P, P], F32)
        make_identity(nc, ident[:])
        warm_in = const.tile([P, 1], F32)
        warm_out = const.tile([P, 1], F32)
        ones = const.tile([P, P], BF16)
        b_row = const.tile([P, H], BF16)
        nc.vector.memset(b_row[:], 0.0)
        nc.vector.memset(ones[:], 1.0)
        nc.vector.memset(warm_in[:], 0.0)
        nc.scalar.activation(out=warm_out[:], in_=warm_in[:], func=TANH)

        w_rows = {
            W_HO: w_ho,
            W_CO: w_co,
            W_C: w_c,
            W_I0: w_i[0:K_PASS, :],
            W_I1: w_i[K_PASS : 2 * K_PASS, :],
        }
        w_raw = {}

        def load_weight(k):
            raw = const.tile([P, PACK * H], BF16, name="w_raw%d" % k)
            nc.sync.dma_start(
                out=raw[:].rearrange("q (u ec) -> q u ec", u=2),
                in_=w_rows[k].rearrange("(u q e) c -> q u (e c)", u=2, e=PAIR),
            )
            w_raw[k] = raw

        chunk_tiles = {}

        def make_chunk(n):
            h_sb = inputs.tile([P, CHUNK_TILES * H], BF16)
            c_sb = inputs.tile([P, CHUNK_TILES * H], BF16)
            x_sb = inputs.tile([P, CHUNK_TILES * D], BF16)
            xz_sb = inputs.tile([P, CHUNK_TILES * H], BF16)
            chunk_tiles[n] = {"h": h_sb, "c": c_sb, "x": x_sb, "xz": xz_sb}

        chunks = {"h": h_chunks, "c": c_chunks, "x": x_chunks, "xz": xz_chunks}

        def load_piece(n, name, piece, pieces):
            sb = chunk_tiles[n][name]
            width = sb.shape[1] // pieces
            cols = slice(piece * width, (piece + 1) * width)
            nc.sync.dma_start(out=sb[:, cols], in_=chunks[name][n, :, cols])

        def load_chunk(n):
            make_chunk(n)
            for name in ("h", "c", "x", "xz"):
                load_piece(n, name, 0, 1)

        load_weight(W_HO)
        load_weight(W_CO)
        make_chunk(0)
        for name in ("h", "c", "x"):
            load_piece(0, name, 0, 2)
        nc.sync.dma_start(out=b_row[0:1, :], in_=b_o.unsqueeze(0))
        load_weight(W_C)
        load_weight(W_I0)
        load_weight(W_I1)
        load_piece(0, "xz", 0, 2)
        for name in ("h", "c", "x", "xz"):
            load_piece(0, name, 1, 2)
        make_chunk(1)
        for piece in range(2):
            for name in ("h", "c", "x", "xz"):
                load_piece(1, name, piece, 2)
        for n in range(2, INPUT_BUFS):
            load_chunk(n)

        w_codes = const.tile([P, W_PASSES * H], U32, align_bytes=256)
        w_scales = const.tile([P, W_PASSES * H], U8, align_bytes=256)
        w_grouped = {}

        def regroup_weight(k):
            wg = w_stage.tile([P, H * PACK], BF16, align_bytes=64)
            rows = w_raw[k][:].rearrange("p (t c) -> p t c", t=PACK)
            nc.vector.tensor_copy(
                out=wg[:, 0 : W_VECTOR_COLS * PACK].rearrange("p (c i t) -> p c t i", i=4, t=PACK),
                in_=rows[:, :, 0:W_VECTOR_COLS].rearrange("p t (c i) -> p c t i", i=4),
            )
            nc.scalar.copy(
                out=wg[:, W_VECTOR_COLS * PACK : H * PACK].rearrange("p (c i t) -> p c t i", i=4, t=PACK),
                in_=rows[:, :, W_VECTOR_COLS:H].rearrange("p t (c i) -> p c t i", i=4),
            )
            w_grouped[k] = wg

        def quantise_weight(k):
            nc.vector.quantize_mx(
                out=w_codes[:, k * H : (k + 1) * H].bitcast(FP8X4),
                scales=w_scales[:, k * H : (k + 1) * H],
                in_=w_grouped[k][:],
            )

        bias = const.tile([P, H], F32)

        def where(i, s):
            return divmod(i * ROUND_TILES + s, CHUNK_TILES)

        banks = {}
        regrouped = {}
        codes = {}
        sums = {}
        biased = {}
        gate_in = {}
        gate = {}

        def add_bias(i):
            pre = gates.tile([P, ROUND_TILES * H], F32)
            for s in range(ROUND_TILES):
                n, t = where(i, s)
                nc.gpsimd.tensor_tensor(
                    out=pre[:, s * H : (s + 1) * H],
                    in0=chunk_tiles[n]["xz"][:, t * H : (t + 1) * H],
                    in1=bias[:],
                    op=ADD,
                )
            biased[i] = pre

        def transpose_round(i):
            h_bank = psum.tile([P, BANK], F32, bufs=1)
            c_bank = psum.tile([P, BANK], F32, bufs=1)
            for name, bank in (("h", h_bank), ("c", c_bank)):
                for s in range(ROUND_TILES):
                    n, t = where(i, s)
                    words = chunk_tiles[n][name][:].bitcast(F32)
                    for u in range(WORDS // P):
                        nc.tensor.transpose(
                            bank[:, (u * ROUND_TILES + s) * P : (u * ROUND_TILES + s + 1) * P],
                            words[:, t * WORDS + u * P : t * WORDS + (u + 1) * P],
                            ident[:],
                        )
            x_banks = []
            for s in range(ROUND_TILES):
                n, t = where(i, s)
                words = chunk_tiles[n]["x"][:].bitcast(F32)
                x_bank = psum.tile([P, BANK], F32)
                for j in range(BANK // P):
                    nc.tensor.transpose(
                        x_bank[:, (j % 2 * 2 + j // 2) * P : (j % 2 * 2 + j // 2 + 1) * P],
                        words[:, t * BANK + j * P : t * BANK + (j + 1) * P],
                        ident[:],
                    )
                x_banks.append(x_bank)
            banks[i] = {"h": h_bank, "c": c_bank, "x": x_banks}

        def interleave(copy, dst_words, bank):
            copy(
                out=dst_words.rearrange("p (w u) -> p w u", u=2),
                in_=bank[:].rearrange("p (u w) -> p w u", u=2),
            )

        def empty_gate_banks(i, copy_h):
            hc_grouped = grouped.tile([P, 2 * ROUND_TILES * K_PASS], BF16, align_bytes=64)
            hc_words = hc_grouped[:].bitcast(F32)
            interleave(copy_h, hc_words[:, 0:BANK], banks[i]["h"])
            interleave(nc.scalar.copy, hc_words[:, BANK : 2 * BANK], banks[i]["c"])
            regrouped[i] = {"hc": hc_grouped}

        def take_tanh_c(i):
            t_grouped = grouped.tile([P, ROUND_TILES * K_PASS], BF16, align_bytes=64)
            c_values = regrouped[i]["hc"][:, ROUND_TILES * K_PASS : 2 * ROUND_TILES * K_PASS]
            nc.scalar.activation(out=t_grouped[:], in_=c_values, func=TANH)
            regrouped[i]["t"] = t_grouped

        def empty_x_banks(i):
            x_grouped = grouped.tile([P, ROUND_TILES * D], BF16, align_bytes=64)
            x_words = x_grouped[:].bitcast(F32)
            interleave(nc.scalar.copy, x_words[:, 0:BANK], banks[i]["x"][0])
            copy = nc.vector.tensor_copy if i % 4 == 0 else nc.scalar.copy
            interleave(copy, x_words[:, BANK : 2 * BANK], banks[i]["x"][1])
            regrouped[i]["x"] = x_grouped

        def quantise_rows(i, name):
            values = regrouped[i][name]
            width = values.shape[1] // PACK
            words = quantised.tile([P, width], U32, name=name + "_codes", align_bytes=256)
            scales = quantised.tile([P, width], U8, name=name + "_scales", align_bytes=256)
            nc.vector.quantize_mx(out=words[:].bitcast(FP8X4), scales=scales[:], in_=values[:])
            codes.setdefault(i, {})[name] = (words, scales)

        def quantise_round(i):
            for name in ("hc", "x", "t"):
                quantise_rows(i, name)

        def mx_pass(bank, operand, block, k, start, stop):
            words, scales = operand
            rows = slice(block * P, (block + 1) * P)
            cols = slice(k * H, (k + 1) * H)
            nc.tensor.matmul_mx(
                out=bank[:],
                lhsT=words[:, rows].bitcast(FP8X4),
                lhsT_scale=scales[:, rows],
                rhs=w_codes[:, cols].bitcast(FP8X4),
                rhs_scale=w_scales[:, cols],
                start=start,
                stop=stop,
            )

        def multiply_gate(i):
            o_banks = []
            for s in range(ROUND_TILES):
                o_bank = psum.tile([P, H], F32)
                mx_pass(o_bank, codes[i]["hc"], s, W_HO, True, False)
                mx_pass(o_bank, codes[i]["hc"], ROUND_TILES + s, W_CO, False, True)
                o_banks.append(o_bank)
            sums[i] = {"o": o_banks}

        def multiply_projections(i):
            r_banks = []
            for s in range(ROUND_TILES):
                r_bank = psum.tile([P, H], F32)
                mx_pass(r_bank, codes[i]["x"], 2 * s, W_I0, True, False)
                mx_pass(r_bank, codes[i]["x"], 2 * s + 1, W_I1, False, False)
                mx_pass(r_bank, codes[i]["t"], s, W_C, False, True)
                r_banks.append(r_bank)
            sums[i]["r"] = r_banks

        def sum_gate_input(i):
            o_sum = gates.tile([P, ROUND_TILES * H], F32)
            for s in range(ROUND_TILES):
                cols = slice(s * H, (s + 1) * H)
                nc.vector.tensor_tensor(out=o_sum[:, cols], in0=sums[i]["o"][s][:], in1=biased[i][:, cols], op=ADD)
            gate_in[i] = o_sum

        def squash_gate(i):
            tanh_o = gates.tile([P, ROUND_TILES * H], F32)
            for s in range(ROUND_TILES):
                cols = slice(s * H, (s + 1) * H)
                nc.scalar.activation(out=tanh_o[:, cols], in_=gate_in[i][:, cols], func=TANH)
            gate[i] = tanh_o

        def finish_round(i):
            product = results.tile([P, ROUND_TILES * H], F32)
            n, t = where(i, 0)
            tiles_a_store = 1 if i == ROUNDS - 1 else ROUND_TILES
            for s in range(ROUND_TILES):
                cols = slice(s * H, (s + 1) * H)
                nc.vector.tensor_tensor(out=product[:, cols], in0=sums[i]["r"][s][:], in1=gate[i][:, cols], op=MULT)
                if (s + 1) % tiles_a_store == 0:
                    first = s + 1 - tiles_a_store
                    nc.sync.dma_start(
                        out=out_chunks[n, :, (t + first) * H : (t + s + 1) * H],
                        in_=product[:, first * H : (s + 1) * H],
                    )

        regroup_weight(W_HO)
        regroup_weight(W_CO)
        quantise_weight(W_HO)
        quantise_weight(W_CO)
        transpose_round(0)
        bias_bank = psum.tile([P, H], F32, tag="r_bank")
        nc.tensor.matmul(out=bias_bank[:], lhsT=ones[:], rhs=b_row[:], start=True, stop=True)
        empty_gate_banks(0, nc.vector.tensor_copy)
        quantise_rows(0, "hc")
        multiply_gate(0)
        take_tanh_c(0)
        regroup_weight(W_C)
        empty_x_banks(0)
        nc.scalar.copy(out=bias[:], in_=bias_bank[:])
        quantise_rows(0, "t")
        regroup_weight(W_I0)
        quantise_weight(W_C)
        quantise_rows(0, "x")
        regroup_weight(W_I1)
        quantise_weight(W_I0)
        quantise_weight(W_I1)
        for i in range(BIAS_AHEAD):
            add_bias(i)
        for i in range(ROUNDS):
            following = i + 1
            if following < ROUNDS:
                transpose_round(following)
            n, t = where(following, ROUND_TILES - 1)
            if t == CHUNK_TILES - 1 and n + INPUT_BUFS < CHUNKS:
                load_chunk(n + INPUT_BUFS)
            if i > 0:
                multiply_gate(i)
            multiply_projections(i)
            if following < ROUNDS:
                empty_gate_banks(following, nc.scalar.copy)
                empty_x_banks(following)
                take_tanh_c(following)
            sum_gate_input(i)
            if following < ROUNDS:
                quantise_round(following)
            squash_gate(i)
            finish_round(i)
            if i + BIAS_AHEAD < ROUNDS:
                add_bias(i + BIAS_AHEAD)
